import numpy as np
import ml_dtypes


def mxq(x, axis, fmt="e4m3"):
    dtype, down = {"e4m3": (ml_dtypes.float8_e4m3fn, 7), "e5m2": (ml_dtypes.float8_e5m2, 14)}[fmt]
    v = np.moveaxis(np.asarray(x, np.float32).astype(ml_dtypes.bfloat16).astype(np.float64), axis, -1)
    blocks = v.reshape(v.shape[:-1] + (-1, 32))
    amax = np.abs(blocks).max(-1, keepdims=True)
    byte = np.maximum(np.where(amax > 0, np.frexp(amax)[1] - 1 + 127, 0) - down, 1)
    scale = np.exp2(byte - 127.0)
    codes = (blocks / scale).astype(np.float32).astype(dtype).astype(np.float64)
    return np.moveaxis((codes * scale).reshape(v.shape), -1, axis)


WIDE = False


def mx_kscale(k):
    if not WIDE:
        return np.ones(k)
    levels = np.array([10, -10, 5, -5, 0])
    a = np.random.permutation(np.resize(levels, k // 512 * 4)).reshape(k // 512, 4)
    idx = np.arange(k)
    return np.exp2(a[idx // 512, idx % 128 // 32])


BF16 = ml_dtypes.bfloat16


def bf(x):
    return np.asarray(x, np.float32).astype(BF16)


def f64(x):
    return np.asarray(x).astype(np.float64)


B, T, E, H, FF = 4, 128, 1024, 8, 4096
EPS = 1e-5


def layernorm(r, g):
    mu = r.mean(-1, keepdims=True)
    var = ((r - mu) ** 2).mean(-1, keepdims=True)
    return (r - mu) / np.sqrt(var + EPS) * g


def silu(v):
    return v / (1.0 + np.exp(-v))


def setup_inputs():
    s = mx_kscale(E)
    return {
        "o": bf(np.random.standard_normal((B, T, E)) * 0.7 * s),
        "x_pos": bf(np.random.standard_normal((B, T, E)) * 1.1 + 0.3),
        "Wo": bf(np.random.standard_normal((E, E)) / np.sqrt(E) / s[:, None]),
        "bo": bf(np.random.standard_normal(E) * 0.1),
        "g1": bf(1.0 + np.random.standard_normal(E) * 0.1),
        "W1": bf(np.random.standard_normal((E, FF)) / np.sqrt(E)),
        "b1": bf(np.random.standard_normal(FF) * 0.1),
    }


def reference(o, x_pos, Wo, bo, g1, W1, b1):
    attn_out = (mxq(f64(o), 2, "e4m3") @ mxq(f64(Wo), 0, "e4m3")) + f64(bo)
    h = layernorm(attn_out + f64(x_pos), f64(g1))
    y = (mxq(h, 2, "e4m3") @ mxq(f64(W1), 0, "e4m3")) + f64(b1)
    act = silu(y) * y
    return h, act

@@ -1,0 +1,251 @@
+from contextlib import ExitStack
+
+import concourse.masks as masks
+import concourse.mybir as mybir
+
+F32 = mybir.dt.float32
+BF16 = mybir.dt.bfloat16
+U32 = mybir.dt.uint32
+U8 = mybir.dt.uint8
+FP8X4 = mybir.dt.float8_e4m3fn_x4
+ALU = mybir.AluOpType
+ACT = mybir.ActivationFunctionType
+
+P = 128
+PACK = 4
+K_PASS = P * PACK
+TILES = 4
+TOKENS = TILES * P
+E = 1024
+FF = 4096
+PASSES = E // K_PASS
+UNIT = 512
+CHUNK = 2 * UNIT
+RUN = 4
+EPS = 1e-5
+
+FLOPS = 2 * TOKENS * E * E + 2 * TOKENS * E * FF
+
+
+def tile_transformerblock_pa_kernel(tc, o, x_pos, Wo, bo, g1, W1, b1, out_0, out_1):
+    nc = tc.nc
+    with ExitStack() as ctx:
+        keep = ctx.enter_context(tc.tile_pool(name="keep", bufs=1))
+        raw_pool = ctx.enter_context(tc.tile_pool(name="raw", bufs=6))
+        stage = ctx.enter_context(tc.tile_pool(name="stage", bufs=4))
+        psum_acc = ctx.enter_context(tc.psum_pool(name="acc", bufs=4))
+        psum_tp = ctx.enter_context(tc.psum_pool(name="tp", bufs=4))
+
+        ident = keep.tile([P, P], F32)
+        masks.make_identity(nc, ident[:])
+
+        def load_wo_pass(g):
+            raw = raw_pool.tile([P, PACK, CHUNK], BF16, tag="raw")
+            for u in range(2):
+                rows = Wo[K_PASS * g + 2 * P * u : K_PASS * g + 2 * P * (u + 1), :]
+                nc.sync.dma_start(out=raw[:, 2 * u : 2 * u + 2, :], in_=rows.rearrange("(q e) c -> q e c", e=2))
+            return raw
+
+        def load_w1_chunk(c, g):
+            raw = raw_pool.tile([P, PACK, CHUNK], BF16, tag="raw")
+            rows = W1[K_PASS * g : K_PASS * (g + 1), CHUNK * c : CHUNK * (c + 1)]
+            nc.sync.dma_start(out=raw[:], in_=rows.rearrange("(t p) n -> p t n", p=P))
+            return raw
+
+        wo_raw = [load_wo_pass(0)]
+        o_sb = keep.tile([P, TILES, E], BF16)
+        nc.sync.dma_start(out=o_sb[:], in_=o.rearrange("b t e -> t b e"))
+        wo_raw.append(load_wo_pass(1))
+        bo_bc = keep.tile([P, E], BF16)
+        nc.sync.dma_start(out=bo_bc[:], in_=bo.partition_broadcast(P))
+        x_sb = keep.tile([P, TILES, E], BF16)
+        nc.sync.dma_start(out=x_sb[:], in_=x_pos.rearrange("b t e -> t b e"))
+        g1_bc = keep.tile([P, E], BF16)
+        nc.sync.dma_start(out=g1_bc[:], in_=g1.partition_broadcast(P))
+        b1_rows = keep.tile([P, P], BF16)
+        nc.vector.memset(b1_rows[:], 0.0)
+        nc.sync.dma_start(out=b1_rows[0 : FF // P, :], in_=b1.rearrange("(c p) -> c p", p=P))
+        w1_raw = {}
+        for c in range(2):
+            for g in range(PASSES):
+                w1_raw[(c, g)] = load_w1_chunk(c, g)
+
+        def quantise_weight_unit(raws, half, codes, scales, cols, scalar_helps):
+            grouped = []
+            for g in range(PASSES):
+                grp = stage.tile([P, UNIT, PACK], BF16, tag="grp", align_bytes=64)
+                src = raws[g][:, :, UNIT * half : UNIT * (half + 1)].rearrange("p t (c i) -> p c t i", i=RUN)
+                dst = grp[:].rearrange("p (c i) t -> p c t i", i=RUN)
+                if scalar_helps and g == 1:
+                    nc.scalar.copy(out=dst, in_=src)
+                else:
+                    nc.vector.tensor_copy(out=dst, in_=src)
+                grouped.append(grp)
+            for g in range(PASSES):
+                nc.vector.quantize_mx(
+                    out=codes[:, g, cols].bitcast(FP8X4),
+                    scales=scales[:, g, cols],
+                    in_=grouped[g][:].rearrange("p c t -> p (c t)"),
+                )
+
+        wo_codes = keep.tile([P, PASSES, E], U32, align_bytes=64)
+        wo_scales = keep.tile([P, PASSES, E], U8, align_bytes=64)
+        w1_codes = keep.tile([P, PASSES, FF], U32, align_bytes=64)
+        w1_scales = keep.tile([P, PASSES, FF], U8, align_bytes=64)
+
+        def quantise_w1_unit(j):
+            c, half = divmod(j, 2)
+            raws = [w1_raw[(c, g)] for g in range(PASSES)]
+            quantise_weight_unit(raws, half, w1_codes, w1_scales, slice(UNIT * j, UNIT * (j + 1)), half == 1)
+            if half == 1 and c + 2 < FF // CHUNK:
+                for g in range(PASSES):
+                    w1_raw[(c + 2, g)] = load_w1_chunk(c + 2, g)
+
+        o_codes = keep.tile([P, TILES, PASSES * P], U32, align_bytes=64)
+        o_scales = keep.tile([P, TILES, PASSES * P], U8, align_bytes=64)
+        for m in range(TILES):
+            o_words = o_sb[:, m, :].bitcast(F32)
+            o_t = psum_tp.tile([P, PASSES * 2, P], F32, tag="tp")
+            for gu in range(PASSES * 2):
+                nc.tensor.transpose(o_t[:, gu, :], o_words[:, P * gu : P * (gu + 1)], ident[:])
+            o_grp = stage.tile([P, PASSES, P, PACK], BF16, tag="o_grp", bufs=2, align_bytes=64)
+            nc.scalar.copy(
+                out=o_grp[:].bitcast(F32),
+                in_=o_t[:].rearrange("p (g u) r -> p g r u", u=2),
+            )
+            nc.vector.quantize_mx(
+                out=o_codes[:, m, :].bitcast(FP8X4),
+                scales=o_scales[:, m, :],
+                in_=o_grp[:].rearrange("p g r t -> p (g r t)"),
+            )
+
+        for n in range(E // UNIT):
+            quantise_weight_unit(wo_raw, n, wo_codes, wo_scales, slice(UNIT * n, UNIT * (n + 1)), n == 1)
+
+        b1_rows_f32 = keep.tile([P, P], F32)
+        nc.vector.tensor_copy(out=b1_rows_f32[:], in_=b1_rows[:])
+        b1_t = psum_tp.tile([P, P], F32, tag="tp")
+        nc.tensor.transpose(b1_t[:], b1_rows_f32[:], ident[:])
+        b1_col = keep.tile([P, FF // P], F32)
+        nc.vector.tensor_copy(out=b1_col[:], in_=b1_t[:, 0 : FF // P])
+
+        resid = keep.tile([P, TILES, E], F32)
+        h_sb = keep.tile([P, TILES, E], F32)
+        row_sum = keep.tile([P, TILES * 2], F32)
+        neg_mean = keep.tile([P, TILES], F32)
+        sq_sum = keep.tile([P, TILES], F32)
+        std = keep.tile([P, TILES], F32)
+        rstd = keep.tile([P, TILES], F32)
+        h_codes = keep.tile([P, PASSES, TOKENS], U32, align_bytes=64)
+        h_scales = keep.tile([P, PASSES, TOKENS], U8, align_bytes=64)
+
+        for m in range(TILES):
+            nc.vector.tensor_tensor(out=resid[:, m, :], in0=x_sb[:, m, :], in1=bo_bc[:], op=ALU.add)
+
+        for m in range(TILES):
+            for n in range(E // UNIT):
+                cols = slice(UNIT * n, UNIT * (n + 1))
+                acc = psum_acc.tile([P, UNIT], F32, tag="acc")
+                for g in range(PASSES):
+                    nc.tensor.matmul_mx(
+                        out=acc[:],
+                        lhsT=o_codes[:, m, P * g : P * (g + 1)].bitcast(FP8X4),
+                        lhsT_scale=o_scales[:, m, P * g : P * (g + 1)],
+                        rhs=wo_codes[:, g, cols].bitcast(FP8X4),
+                        rhs_scale=wo_scales[:, g, cols],
+                        start=(g == 0),
+                        stop=(g == PASSES - 1),
+                    )
+                nc.vector.scalar_tensor_tensor(
+                    out=resid[:, m, cols],
+                    in0=acc[:],
+                    scalar=0.0,
+                    in1=resid[:, m, cols],
+                    op0=ALU.add,
+                    op1=ALU.add,
+                    accum_out=row_sum[:, 2 * m + n : 2 * m + n + 1],
+                )
+            nc.vector.tensor_scalar(
+                out=neg_mean[:, m : m + 1],
+                in0=row_sum[:, 2 * m : 2 * m + 1],
+                scalar1=row_sum[:, 2 * m + 1 : 2 * m + 2],
+                scalar2=-1.0 / E,
+                op0=ALU.add,
+                op1=ALU.mult,
+            )
+            squares = stage.tile([P, E], BF16, tag="squares", bufs=2)
+            nc.scalar.activation(
+                out=squares[:],
+                in_=resid[:, m, :],
+                func=ACT.Square,
+                bias=neg_mean[:, m : m + 1],
+                scale=1.0,
+                accum_out=sq_sum[:, m : m + 1],
+            )
+            nc.vector.scalar_tensor_tensor(
+                out=h_sb[:, m, :],
+                in0=resid[:, m, :],
+                scalar=neg_mean[:, m : m + 1],
+                in1=g1_bc[:],
+                op0=ALU.add,
+                op1=ALU.mult,
+            )
+            nc.scalar.activation(
+                out=std[:, m : m + 1], in_=sq_sum[:, m : m + 1], func=ACT.Sqrt, bias=EPS, scale=1.0 / E
+            )
+            nc.vector.reciprocal(out=rstd[:, m : m + 1], in_=std[:, m : m + 1])
+            nc.scalar.activation(out=h_sb[:, m, :], in_=h_sb[:, m, :], func=ACT.Copy, scale=rstd[:, m : m + 1])
+            nc.sync.dma_start(out=out_0[m, :, :], in_=h_sb[:, m, :])
+
+            for g in range(PASSES):
+                h_t = psum_tp.tile([P, PACK, P], F32, tag="tp")
+                for t in range(PACK):
+                    k0 = K_PASS * g + P * t
+                    nc.tensor.transpose(h_t[:, t, :], h_sb[:, m, k0 : k0 + P], ident[:])
+                h_grp = stage.tile([P, P, PACK], BF16, tag="h_grp", align_bytes=64)
+                nc.scalar.copy(out=h_grp[:], in_=h_t[:].rearrange("p t r -> p r t"))
+                nc.vector.quantize_mx(
+                    out=h_codes[:, g, P * m : P * (m + 1)].bitcast(FP8X4),
+                    scales=h_scales[:, g, P * m : P * (m + 1)],
+                    in_=h_grp[:].rearrange("p r t -> p (r t)"),
+                )
+
+        quantise_w1_unit(0)
+        quantise_w1_unit(1)
+        for j in range(FF // UNIT):
+            if j + 2 < FF // UNIT:
+                quantise_w1_unit(j + 2)
+            gated = []
+            for f in range(UNIT // P):
+                col = (UNIT // P) * j + f
+                cols = slice(P * col, P * (col + 1))
+                y_t = psum_acc.tile([P, TOKENS], F32, tag="acc")
+                for g in range(PASSES):
+                    nc.tensor.matmul_mx(
+                        out=y_t[:],
+                        lhsT=w1_codes[:, g, cols].bitcast(FP8X4),
+                        lhsT_scale=w1_scales[:, g, cols],
+                        rhs=h_codes[:, g, :].bitcast(FP8X4),
+                        rhs_scale=h_scales[:, g, :],
+                        start=(g == 0),
+                        stop=(g == PASSES - 1),
+                    )
+                sil = stage.tile([P, TOKENS], F32, tag="sil")
+                nc.scalar.activation(out=sil[:], in_=y_t[:], func=ACT.Silu, bias=b1_col[:, col : col + 1], scale=1.0)
+                gate = stage.tile([P, TOKENS], F32, tag="gate", bufs=8)
+                nc.vector.scalar_tensor_tensor(
+                    out=gate[:],
+                    in0=y_t[:],
+                    scalar=b1_col[:, col : col + 1],
+                    in1=sil[:],
+                    op0=ALU.add,
+                    op1=ALU.mult,
+                )
+                gated.append(gate)
+            for m in range(TILES):
+                act_t = psum_tp.tile([P, UNIT], F32, tag="tp")
+                for f in range(UNIT // P):
+                    nc.tensor.transpose(act_t[:, P * f : P * (f + 1)], gated[f][:, P * m : P * (m + 1)], ident[:])
+                act_sb = stage.tile([P, UNIT], F32, tag="act_sb", bufs=6)
+                nc.scalar.copy(out=act_sb[:], in_=act_t[:])
+                nc.sync.dma_start(out=out_1[m, :, UNIT * j : UNIT * (j + 1)], in_=act_sb[:])

@@ -19,9 +19,15 @@ TOKENS = TILES * P
 E = 1024
 FF = 4096
 PASSES = E // K_PASS
-UNIT = 512
-CHUNK = 2 * UNIT
+BANK = 512
+CHUNK = 1024
 RUN = 4
+SCALAR_COLS = 256
+ROUNDS = FF // BANK
+BLOCKS = BANK // P
+W1_CHUNKS = PASSES * FF // CHUNK
+RAW_BUFS = 6
+LEAD = 3
 EPS = 1e-5
 
 FLOPS = 2 * TOKENS * E * E + 2 * TOKENS * E * FF
@@ -30,8 +36,9 @@ FLOPS = 2 * TOKENS * E * E + 2 * TOKENS * E * FF
 def tile_transformerblock_pa_kernel(tc, o, x_pos, Wo, bo, g1, W1, b1, out_0, out_1):
     nc = tc.nc
     with ExitStack() as ctx:
+        ctx.enter_context(tc.manual_schedule())
         keep = ctx.enter_context(tc.tile_pool(name="keep", bufs=1))
-        raw_pool = ctx.enter_context(tc.tile_pool(name="raw", bufs=6))
+        raw_pool = ctx.enter_context(tc.tile_pool(name="raw", bufs=RAW_BUFS))
         stage = ctx.enter_context(tc.tile_pool(name="stage", bufs=4))
         psum_acc = ctx.enter_context(tc.psum_pool(name="acc", bufs=4))
         psum_tp = ctx.enter_context(tc.psum_pool(name="tp", bufs=4))
@@ -46,88 +53,97 @@ def tile_transformerblock_pa_kernel(tc, o, x_pos, Wo, bo, g1, W1, b1, out_0, out
                 nc.sync.dma_start(out=raw[:, 2 * u : 2 * u + 2, :], in_=rows.rearrange("(q e) c -> q e c", e=2))
             return raw
 
-        def load_w1_chunk(c, g):
-            raw = raw_pool.tile([P, PACK, CHUNK], BF16, tag="raw")
-            rows = W1[K_PASS * g : K_PASS * (g + 1), CHUNK * c : CHUNK * (c + 1)]
-            nc.sync.dma_start(out=raw[:], in_=rows.rearrange("(t p) n -> p t n", p=P))
-            return raw
+        w1_raw = {}
 
-        wo_raw = [load_wo_pass(0)]
+        def load_w1_chunk(i):
+            if i < W1_CHUNKS:
+                c, g = divmod(i, PASSES)
+                raw = raw_pool.tile([P, PACK, CHUNK], BF16, tag="raw")
+                rows = W1[K_PASS * g : K_PASS * (g + 1), CHUNK * c : CHUNK * (c + 1)]
+                nc.sync.dma_start(out=raw[:], in_=rows.rearrange("(t p) n -> p t n", p=P))
+                w1_raw[i] = raw
+
         o_sb = keep.tile([P, TILES, E], BF16)
-        nc.sync.dma_start(out=o_sb[:], in_=o.rearrange("b t e -> t b e"))
-        wo_raw.append(load_wo_pass(1))
-        bo_bc = keep.tile([P, E], BF16)
-        nc.sync.dma_start(out=bo_bc[:], in_=bo.partition_broadcast(P))
         x_sb = keep.tile([P, TILES, E], BF16)
-        nc.sync.dma_start(out=x_sb[:], in_=x_pos.rearrange("b t e -> t b e"))
+        bo_bc = keep.tile([P, E], BF16)
         g1_bc = keep.tile([P, E], BF16)
-        nc.sync.dma_start(out=g1_bc[:], in_=g1.partition_broadcast(P))
         b1_rows = keep.tile([P, P], BF16)
         nc.vector.memset(b1_rows[:], 0.0)
-        nc.sync.dma_start(out=b1_rows[0 : FF // P, :], in_=b1.rearrange("(c p) -> c p", p=P))
-        w1_raw = {}
-        for c in range(2):
-            for g in range(PASSES):
-                w1_raw[(c, g)] = load_w1_chunk(c, g)
 
-        def quantise_weight_unit(raws, half, codes, scales, cols, scalar_helps):
-            grouped = []
-            for g in range(PASSES):
-                grp = stage.tile([P, UNIT, PACK], BF16, tag="grp", align_bytes=64)
-                src = raws[g][:, :, UNIT * half : UNIT * (half + 1)].rearrange("p t (c i) -> p c t i", i=RUN)
-                dst = grp[:].rearrange("p (c i) t -> p c t i", i=RUN)
-                if scalar_helps and g == 1:
-                    nc.scalar.copy(out=dst, in_=src)
-                else:
-                    nc.vector.tensor_copy(out=dst, in_=src)
-                grouped.append(grp)
-            for g in range(PASSES):
-                nc.vector.quantize_mx(
-                    out=codes[:, g, cols].bitcast(FP8X4),
-                    scales=scales[:, g, cols],
-                    in_=grouped[g][:].rearrange("p c t -> p (c t)"),
-                )
+        nc.sync.dma_start(out=b1_rows[0 : FF // P, :], in_=b1.rearrange("(c p) -> c p", p=P))
+        wo_raw = [load_wo_pass(0), load_wo_pass(1)]
+        nc.sync.dma_start(out=o_sb[:, 0, :], in_=o[0, :, :])
+        nc.sync.dma_start(out=bo_bc[:], in_=bo.partition_broadcast(P))
+        nc.sync.dma_start(out=x_sb[:, 0, :], in_=x_pos[0, :, :])
+        nc.sync.dma_start(out=g1_bc[:], in_=g1.partition_broadcast(P))
+        for m in range(1, TILES):
+            nc.sync.dma_start(out=o_sb[:, m, :], in_=o[m, :, :])
+            nc.sync.dma_start(out=x_sb[:, m, :], in_=x_pos[m, :, :])
+        for i in range(RAW_BUFS - PASSES):
+            load_w1_chunk(i)
 
         wo_codes = keep.tile([P, PASSES, E], U32, align_bytes=64)
         wo_scales = keep.tile([P, PASSES, E], U8, align_bytes=64)
         w1_codes = keep.tile([P, PASSES, FF], U32, align_bytes=64)
         w1_scales = keep.tile([P, PASSES, FF], U8, align_bytes=64)
 
-        def quantise_w1_unit(j):
-            c, half = divmod(j, 2)
-            raws = [w1_raw[(c, g)] for g in range(PASSES)]
-            quantise_weight_unit(raws, half, w1_codes, w1_scales, slice(UNIT * j, UNIT * (j + 1)), half == 1)
-            if half == 1 and c + 2 < FF // CHUNK:
-                for g in range(PASSES):
-                    w1_raw[(c + 2, g)] = load_w1_chunk(c + 2, g)
+        def regroup(raw):
+            grp = stage.tile([P, CHUNK, PACK], BF16, tag="grp", bufs=3, align_bytes=64)
+            split = CHUNK - SCALAR_COLS
+            nc.vector.tensor_copy(
+                out=grp[:, :split, :].rearrange("p (c i) t -> p c t i", i=RUN),
+                in_=raw[:, :, :split].rearrange("p t (c i) -> p c t i", i=RUN),
+            )
+            nc.scalar.copy(
+                out=grp[:, split:, :].rearrange("p (c i) t -> p c t i", i=RUN),
+                in_=raw[:, :, split:].rearrange("p t (c i) -> p c t i", i=RUN),
+            )
+            return grp
+
+        def quantise(grp, codes, scales):
+            nc.vector.quantize_mx(out=codes.bitcast(FP8X4), scales=scales, in_=grp[:].rearrange("p c t -> p (c t)"))
+
+        w1_grp = {}
+
+        def regroup_w1(i):
+            w1_grp[i] = regroup(w1_raw[i])
+            load_w1_chunk(i + RAW_BUFS)
+
+        def quantise_w1(i):
+            c, g = divmod(i, PASSES)
+            cols = slice(CHUNK * c, CHUNK * (c + 1))
+            quantise(w1_grp[i], w1_codes[:, g, cols], w1_scales[:, g, cols])
+
+        def spread_b1():
+            b1_rows_f32 = keep.tile([P, P], F32)
+            nc.vector.tensor_copy(out=b1_rows_f32[:], in_=b1_rows[:])
+            b1_t = psum_tp.tile([P, P], F32, tag="tp")
+            nc.tensor.transpose(b1_t[:], b1_rows_f32[:], ident[:])
+            nc.vector.tensor_copy(out=b1_col[:], in_=b1_t[:, 0 : FF // P])
+
+        b1_col = keep.tile([P, FF // P], F32)
 
         o_codes = keep.tile([P, TILES, PASSES * P], U32, align_bytes=64)
         o_scales = keep.tile([P, TILES, PASSES * P], U8, align_bytes=64)
-        for m in range(TILES):
+        o_t = {}
+        o_grp = {}
+
+        def transpose_o(m):
             o_words = o_sb[:, m, :].bitcast(F32)
-            o_t = psum_tp.tile([P, PASSES * 2, P], F32, tag="tp")
+            o_t[m] = psum_tp.tile([P, PASSES * 2, P], F32, tag="tp", name="o_t")
             for gu in range(PASSES * 2):
-                nc.tensor.transpose(o_t[:, gu, :], o_words[:, P * gu : P * (gu + 1)], ident[:])
-            o_grp = stage.tile([P, PASSES, P, PACK], BF16, tag="o_grp", bufs=2, align_bytes=64)
-            nc.scalar.copy(
-                out=o_grp[:].bitcast(F32),
-                in_=o_t[:].rearrange("p (g u) r -> p g r u", u=2),
-            )
+                nc.tensor.transpose(o_t[m][:, gu, :], o_words[:, P * gu : P * (gu + 1)], ident[:])
+
+        def copy_out_o(m):
+            o_grp[m] = stage.tile([P, PASSES, P, PACK], BF16, tag="o_grp", bufs=2, align_bytes=64, name="o_grp")
+            nc.scalar.copy(out=o_grp[m][:].bitcast(F32), in_=o_t[m][:].rearrange("p (g u) r -> p g r u", u=2))
+
+        def quantise_o(m):
             nc.vector.quantize_mx(
                 out=o_codes[:, m, :].bitcast(FP8X4),
                 scales=o_scales[:, m, :],
-                in_=o_grp[:].rearrange("p g r t -> p (g r t)"),
+                in_=o_grp[m][:].rearrange("p g r t -> p (g r t)"),
             )
-
-        for n in range(E // UNIT):
-            quantise_weight_unit(wo_raw, n, wo_codes, wo_scales, slice(UNIT * n, UNIT * (n + 1)), n == 1)
-
-        b1_rows_f32 = keep.tile([P, P], F32)
-        nc.vector.tensor_copy(out=b1_rows_f32[:], in_=b1_rows[:])
-        b1_t = psum_tp.tile([P, P], F32, tag="tp")
-        nc.tensor.transpose(b1_t[:], b1_rows_f32[:], ident[:])
-        b1_col = keep.tile([P, FF // P], F32)
-        nc.vector.tensor_copy(out=b1_col[:], in_=b1_t[:, 0 : FF // P])
 
         resid = keep.tile([P, TILES, E], F32)
         h_sb = keep.tile([P, TILES, E], F32)
@@ -138,17 +154,20 @@ def tile_transformerblock_pa_kernel(tc, o, x_pos, Wo, bo, g1, W1, b1, out_0, out
         rstd = keep.tile([P, TILES], F32)
         h_codes = keep.tile([P, PASSES, TOKENS], U32, align_bytes=64)
         h_scales = keep.tile([P, PASSES, TOKENS], U8, align_bytes=64)
+        acc = {}
+        h_t = {}
+        h_grp = {}
 
-        for m in range(TILES):
+        def add_bias_to_residual(m):
             nc.vector.tensor_tensor(out=resid[:, m, :], in0=x_sb[:, m, :], in1=bo_bc[:], op=ALU.add)
 
-        for m in range(TILES):
-            for n in range(E // UNIT):
-                cols = slice(UNIT * n, UNIT * (n + 1))
-                acc = psum_acc.tile([P, UNIT], F32, tag="acc")
+        def first_product(m):
+            for n in range(E // BANK):
+                cols = slice(BANK * n, BANK * (n + 1))
+                acc[(m, n)] = psum_acc.tile([P, BANK], F32, tag="acc", name="acc")
                 for g in range(PASSES):
                     nc.tensor.matmul_mx(
-                        out=acc[:],
+                        out=acc[(m, n)][:],
                         lhsT=o_codes[:, m, P * g : P * (g + 1)].bitcast(FP8X4),
                         lhsT_scale=o_scales[:, m, P * g : P * (g + 1)],
                         rhs=wo_codes[:, g, cols].bitcast(FP8X4),
@@ -156,9 +175,13 @@ def tile_transformerblock_pa_kernel(tc, o, x_pos, Wo, bo, g1, W1, b1, out_0, out
                         start=(g == 0),
                         stop=(g == PASSES - 1),
                     )
+
+        def residual_and_mean(m):
+            for n in range(E // BANK):
+                cols = slice(BANK * n, BANK * (n + 1))
                 nc.vector.scalar_tensor_tensor(
                     out=resid[:, m, cols],
-                    in0=acc[:],
+                    in0=acc[(m, n)][:],
                     scalar=0.0,
                     in1=resid[:, m, cols],
                     op0=ALU.add,
@@ -173,7 +196,9 @@ def tile_transformerblock_pa_kernel(tc, o, x_pos, Wo, bo, g1, W1, b1, out_0, out
                 op0=ALU.add,
                 op1=ALU.mult,
             )
-            squares = stage.tile([P, E], BF16, tag="squares", bufs=2)
+
+        def standard_deviation(m):
+            squares = stage.tile([P, E], BF16, tag="squares", bufs=1)
             nc.scalar.activation(
                 out=squares[:],
                 in_=resid[:, m, :],
@@ -182,6 +207,11 @@ def tile_transformerblock_pa_kernel(tc, o, x_pos, Wo, bo, g1, W1, b1, out_0, out
                 scale=1.0,
                 accum_out=sq_sum[:, m : m + 1],
             )
+            nc.scalar.activation(
+                out=std[:, m : m + 1], in_=sq_sum[:, m : m + 1], func=ACT.Sqrt, bias=EPS, scale=1.0 / E
+            )
+
+        def centre_and_gain(m):
             nc.vector.scalar_tensor_tensor(
                 out=h_sb[:, m, :],
                 in0=resid[:, m, :],
@@ -190,39 +220,42 @@ def tile_transformerblock_pa_kernel(tc, o, x_pos, Wo, bo, g1, W1, b1, out_0, out
                 op0=ALU.add,
                 op1=ALU.mult,
             )
-            nc.scalar.activation(
-                out=std[:, m : m + 1], in_=sq_sum[:, m : m + 1], func=ACT.Sqrt, bias=EPS, scale=1.0 / E
-            )
-            nc.vector.reciprocal(out=rstd[:, m : m + 1], in_=std[:, m : m + 1])
+
+        def finish_h(m):
             nc.scalar.activation(out=h_sb[:, m, :], in_=h_sb[:, m, :], func=ACT.Copy, scale=rstd[:, m : m + 1])
             nc.sync.dma_start(out=out_0[m, :, :], in_=h_sb[:, m, :])
 
+        def transpose_h(m):
             for g in range(PASSES):
-                h_t = psum_tp.tile([P, PACK, P], F32, tag="tp")
+                h_t[(m, g)] = psum_tp.tile([P, PACK, P], F32, tag="tp", name="h_t")
                 for t in range(PACK):
                     k0 = K_PASS * g + P * t
-                    nc.tensor.transpose(h_t[:, t, :], h_sb[:, m, k0 : k0 + P], ident[:])
-                h_grp = stage.tile([P, P, PACK], BF16, tag="h_grp", align_bytes=64)
-                nc.scalar.copy(out=h_grp[:], in_=h_t[:].rearrange("p t r -> p r t"))
+                    nc.tensor.transpose(h_t[(m, g)][:, t, :], h_sb[:, m, k0 : k0 + P], ident[:])
+
+        def copy_out_h(m):
+            for g in range(PASSES):
+                h_grp[(m, g)] = stage.tile([P, P, PACK], BF16, tag="h_grp", align_bytes=64, name="h_grp")
+                nc.scalar.copy(out=h_grp[(m, g)][:], in_=h_t[(m, g)][:].rearrange("p t r -> p r t"))
+
+        def quantise_h(m):
+            for g in range(PASSES):
                 nc.vector.quantize_mx(
                     out=h_codes[:, g, P * m : P * (m + 1)].bitcast(FP8X4),
                     scales=h_scales[:, g, P * m : P * (m + 1)],
-                    in_=h_grp[:].rearrange("p r t -> p (r t)"),
+                    in_=h_grp[(m, g)][:].rearrange("p r t -> p (r t)"),
                 )
 
-        quantise_w1_unit(0)
-        quantise_w1_unit(1)
-        for j in range(FF // UNIT):
-            if j + 2 < FF // UNIT:
-                quantise_w1_unit(j + 2)
-            gated = []
-            for f in range(UNIT // P):
-                col = (UNIT // P) * j + f
-                cols = slice(P * col, P * (col + 1))
-                y_t = psum_acc.tile([P, TOKENS], F32, tag="acc")
+        y_t = {}
+        gated = {}
+        act_t = {}
+
+        def second_product(j):
+            for f in range(BLOCKS):
+                cols = slice(BANK * j + P * f, BANK * j + P * (f + 1))
+                y_t[(j, f)] = psum_acc.tile([P, TOKENS], F32, tag="acc", name="y_t")
                 for g in range(PASSES):
                     nc.tensor.matmul_mx(
-                        out=y_t[:],
+                        out=y_t[(j, f)][:],
                         lhsT=w1_codes[:, g, cols].bitcast(FP8X4),
                         lhsT_scale=w1_scales[:, g, cols],
                         rhs=h_codes[:, g, :].bitcast(FP8X4),
@@ -230,22 +263,87 @@ def tile_transformerblock_pa_kernel(tc, o, x_pos, Wo, bo, g1, W1, b1, out_0, out
                         start=(g == 0),
                         stop=(g == PASSES - 1),
                     )
+
+        def gate(j):
+            for f in range(BLOCKS):
+                bias = b1_col[:, BLOCKS * j + f : BLOCKS * j + f + 1]
                 sil = stage.tile([P, TOKENS], F32, tag="sil")
-                nc.scalar.activation(out=sil[:], in_=y_t[:], func=ACT.Silu, bias=b1_col[:, col : col + 1], scale=1.0)
-                gate = stage.tile([P, TOKENS], F32, tag="gate", bufs=8)
+                nc.scalar.activation(out=sil[:], in_=y_t[(j, f)][:], func=ACT.Silu, bias=bias, scale=1.0)
+                gated[(j, f)] = stage.tile([P, TOKENS], F32, tag="gated", bufs=6, name="gated")
                 nc.vector.scalar_tensor_tensor(
-                    out=gate[:],
-                    in0=y_t[:],
-                    scalar=b1_col[:, col : col + 1],
-                    in1=sil[:],
-                    op0=ALU.add,
-                    op1=ALU.mult,
+                    out=gated[(j, f)][:], in0=y_t[(j, f)][:], scalar=bias, in1=sil[:], op0=ALU.add, op1=ALU.mult
                 )
-                gated.append(gate)
+
+        def turn_back(j):
             for m in range(TILES):
-                act_t = psum_tp.tile([P, UNIT], F32, tag="tp")
-                for f in range(UNIT // P):
-                    nc.tensor.transpose(act_t[:, P * f : P * (f + 1)], gated[f][:, P * m : P * (m + 1)], ident[:])
-                act_sb = stage.tile([P, UNIT], F32, tag="act_sb", bufs=6)
-                nc.scalar.copy(out=act_sb[:], in_=act_t[:])
-                nc.sync.dma_start(out=out_1[m, :, UNIT * j : UNIT * (j + 1)], in_=act_sb[:])
+                act_t[(j, m)] = psum_tp.tile([P, BANK], F32, tag="tp", name="act_t")
+                for f in range(BLOCKS):
+                    nc.tensor.transpose(
+                        act_t[(j, m)][:, P * f : P * (f + 1)], gated[(j, f)][:, P * m : P * (m + 1)], ident[:]
+                    )
+
+        def store_act(j, vector_helps):
+            for m in range(TILES):
+                act_sb = stage.tile([P, BANK], F32, tag="act_sb", bufs=6)
+                if vector_helps and m % 2 == 1:
+                    nc.vector.tensor_copy(out=act_sb[:], in_=act_t[(j, m)][:])
+                else:
+                    nc.scalar.copy(out=act_sb[:], in_=act_t[(j, m)][:])
+                nc.sync.dma_start(out=out_1[m, :, BANK * j : BANK * (j + 1)], in_=act_sb[:])
+
+        spread_b1()
+        wo_grp = [regroup(wo_raw[0])]
+        load_w1_chunk(RAW_BUFS - PASSES)
+        quantise(wo_grp[0], wo_codes[:, 0, :], wo_scales[:, 0, :])
+        wo_grp.append(regroup(wo_raw[1]))
+        load_w1_chunk(RAW_BUFS - PASSES + 1)
+        for m in range(TILES):
+            transpose_o(m)
+        copy_out_o(0)
+        copy_out_o(1)
+        quantise(wo_grp[1], wo_codes[:, 1, :], wo_scales[:, 1, :])
+        for m in range(2):
+            quantise_o(m)
+            add_bias_to_residual(m)
+            first_product(m)
+            copy_out_o(m + 2)
+
+        for m in range(TILES + 1):
+            if m < TILES:
+                residual_and_mean(m)
+                standard_deviation(m)
+                centre_and_gain(m)
+            if m + 2 < TILES:
+                quantise_o(m + 2)
+                add_bias_to_residual(m + 2)
+                first_product(m + 2)
+            else:
+                regroup_w1(m + 2 - TILES)
+            if m < TILES:
+                nc.vector.reciprocal(out=rstd[:, m : m + 1], in_=std[:, m : m + 1])
+            if m >= 1:
+                copy_out_h(m - 1)
+            if m < TILES:
+                finish_h(m)
+                transpose_h(m)
+            if m + 1 >= TILES:
+                quantise_w1(m + 1 - TILES)
+            if m >= 1:
+                quantise_h(m - 1)
+        regroup_w1(LEAD)
+        quantise_w1(LEAD - 1)
+
+        second_product(0)
+        for j in range(ROUNDS):
+            weights_left = j + LEAD < W1_CHUNKS
+            gate(j)
+            if j + 1 < ROUNDS:
+                second_product(j + 1)
+            if j >= 1:
+                store_act(j - 1, not weights_left)
+            turn_back(j)
+            if weights_left:
+                quantise_w1(j + LEAD)
+            if j + LEAD + 1 < W1_CHUNKS:
+                regroup_w1(j + LEAD + 1)
+        store_act(ROUNDS - 1, True)

@@ -36,7 +36,6 @@ FLOPS = 2 * TOKENS * E * E + 2 * TOKENS * E * FF
 def tile_transformerblock_pa_kernel(tc, o, x_pos, Wo, bo, g1, W1, b1, out_0, out_1):
     nc = tc.nc
     with ExitStack() as ctx:
-        ctx.enter_context(tc.manual_schedule())
         keep = ctx.enter_context(tc.tile_pool(name="keep", bufs=1))
         raw_pool = ctx.enter_context(tc.tile_pool(name="raw", bufs=RAW_BUFS))
         stage = ctx.enter_context(tc.tile_pool(name="stage", bufs=4))

@@ -64,18 +64,16 @@ def tile_transformerblock_pa_kernel(tc, o, x_pos, Wo, bo, g1, W1, b1, out_0, out
 
         o_sb = keep.tile([P, TILES, E], BF16)
         x_sb = keep.tile([P, TILES, E], BF16)
-        bo_bc = keep.tile([P, E], BF16)
-        g1_bc = keep.tile([P, E], BF16)
         b1_rows = keep.tile([P, P], BF16)
         nc.vector.memset(b1_rows[:], 0.0)
+        vec_rows = keep.tile([P, 2, E], BF16)
+        nc.vector.memset(vec_rows[:], 0.0)
 
+        nc.sync.dma_start(out=vec_rows[0:1, 0, :], in_=bo.rearrange("(a e) -> a e", a=1))
+        nc.sync.dma_start(out=vec_rows[0:1, 1, :], in_=g1.rearrange("(a e) -> a e", a=1))
         nc.sync.dma_start(out=b1_rows[0 : FF // P, :], in_=b1.rearrange("(c p) -> c p", p=P))
         wo_raw = [load_wo_pass(0), load_wo_pass(1)]
-        nc.sync.dma_start(out=o_sb[:, 0, :], in_=o[0, :, :])
-        nc.sync.dma_start(out=bo_bc[:], in_=bo.partition_broadcast(P))
-        nc.sync.dma_start(out=x_sb[:, 0, :], in_=x_pos[0, :, :])
-        nc.sync.dma_start(out=g1_bc[:], in_=g1.partition_broadcast(P))
-        for m in range(1, TILES):
+        for m in range(TILES):
             nc.sync.dma_start(out=o_sb[:, m, :], in_=o[m, :, :])
             nc.sync.dma_start(out=x_sb[:, m, :], in_=x_pos[m, :, :])
         for i in range(RAW_BUFS - PASSES):
@@ -113,6 +111,19 @@ def tile_transformerblock_pa_kernel(tc, o, x_pos, Wo, bo, g1, W1, b1, out_0, out
             cols = slice(CHUNK * c, CHUNK * (c + 1))
             quantise(w1_grp[i], w1_codes[:, g, cols], w1_scales[:, g, cols])
 
+        ones = keep.tile([P, P], BF16)
+        nc.vector.memset(ones[:], 1.0)
+        ident_bf16 = keep.tile([P, P], BF16)
+        masks.make_identity(nc, ident_bf16[:])
+        g1_bc = keep.tile([P, E], BF16)
+
+        def spread_g1():
+            for n in range(E // BANK):
+                cols = slice(BANK * n, BANK * (n + 1))
+                spread = psum_tp.tile([P, BANK], F32, tag="tp")
+                nc.tensor.matmul(out=spread[:], lhsT=ones[:], rhs=vec_rows[:, 1, cols], start=True, stop=True)
+                nc.scalar.copy(out=g1_bc[:, cols], in_=spread[:])
+
         def spread_b1():
             b1_rows_f32 = keep.tile([P, P], F32)
             nc.vector.tensor_copy(out=b1_rows_f32[:], in_=b1_rows[:])
@@ -149,7 +160,6 @@ def tile_transformerblock_pa_kernel(tc, o, x_pos, Wo, bo, g1, W1, b1, out_0, out
         row_sum = keep.tile([P, TILES * 2], F32)
         neg_mean = keep.tile([P, TILES], F32)
         sq_sum = keep.tile([P, TILES], F32)
-        std = keep.tile([P, TILES], F32)
         rstd = keep.tile([P, TILES], F32)
         h_codes = keep.tile([P, PASSES, TOKENS], U32, align_bytes=64)
         h_scales = keep.tile([P, PASSES, TOKENS], U8, align_bytes=64)
@@ -158,7 +168,12 @@ def tile_transformerblock_pa_kernel(tc, o, x_pos, Wo, bo, g1, W1, b1, out_0, out
         h_grp = {}
 
         def add_bias_to_residual(m):
-            nc.vector.tensor_tensor(out=resid[:, m, :], in0=x_sb[:, m, :], in1=bo_bc[:], op=ALU.add)
+            for n in range(E // BANK):
+                cols = slice(BANK * n, BANK * (n + 1))
+                x_bo = psum_tp.tile([P, BANK], F32, tag="tp")
+                nc.tensor.matmul(out=x_bo[:], lhsT=ident_bf16[:], rhs=x_sb[:, m, cols], start=True, stop=False)
+                nc.tensor.matmul(out=x_bo[:], lhsT=ones[:], rhs=vec_rows[:, 0, cols], start=False, stop=True)
+                nc.scalar.copy(out=resid[:, m, cols], in_=x_bo[:])
 
         def first_product(m):
             for n in range(E // BANK):
@@ -196,7 +211,7 @@ def tile_transformerblock_pa_kernel(tc, o, x_pos, Wo, bo, g1, W1, b1, out_0, out
                 op1=ALU.mult,
             )
 
-        def standard_deviation(m):
+        def reciprocal_deviation(m):
             squares = stage.tile([P, E], BF16, tag="squares", bufs=1)
             nc.scalar.activation(
                 out=squares[:],
@@ -207,7 +222,11 @@ def tile_transformerblock_pa_kernel(tc, o, x_pos, Wo, bo, g1, W1, b1, out_0, out
                 accum_out=sq_sum[:, m : m + 1],
             )
             nc.scalar.activation(
-                out=std[:, m : m + 1], in_=sq_sum[:, m : m + 1], func=ACT.Sqrt, bias=EPS, scale=1.0 / E
+                out=rstd[:, m : m + 1],
+                in_=sq_sum[:, m : m + 1],
+                func=ACT.Abs_reciprocal_sqrt,
+                bias=EPS,
+                scale=1.0 / E,
             )
 
         def centre_and_gain(m):
@@ -283,13 +302,22 @@ def tile_transformerblock_pa_kernel(tc, o, x_pos, Wo, bo, g1, W1, b1, out_0, out
 
         def store_act(j, vector_helps):
             for m in range(TILES):
-                act_sb = stage.tile([P, BANK], F32, tag="act_sb", bufs=6)
+                act_sb = stage.tile([P, BANK], F32, tag="act_sb", bufs=8)
                 if vector_helps and m % 2 == 1:
                     nc.vector.tensor_copy(out=act_sb[:], in_=act_t[(j, m)][:])
                 else:
                     nc.scalar.copy(out=act_sb[:], in_=act_t[(j, m)][:])
                 nc.sync.dma_start(out=out_1[m, :, BANK * j : BANK * (j + 1)], in_=act_sb[:])
 
+        one = keep.tile([P, 1], F32)
+        nc.vector.memset(one[:], 1.0)
+        unused = keep.tile([P, 1], F32)
+
+        def warm_up(func, column):
+            nc.scalar.activation(out=unused[:], in_=column, func=func)
+
+        warm_up(ACT.Abs_reciprocal_sqrt, one[:])
+        spread_g1()
         spread_b1()
         wo_grp = [regroup(wo_raw[0])]
         load_w1_chunk(RAW_BUFS - PASSES)
@@ -310,7 +338,7 @@ def tile_transformerblock_pa_kernel(tc, o, x_pos, Wo, bo, g1, W1, b1, out_0, out
         for m in range(TILES + 1):
             if m < TILES:
                 residual_and_mean(m)
-                standard_deviation(m)
+                reciprocal_deviation(m)
                 centre_and_gain(m)
             if m + 2 < TILES:
                 quantise_o(m + 2)
@@ -318,13 +346,13 @@ def tile_transformerblock_pa_kernel(tc, o, x_pos, Wo, bo, g1, W1, b1, out_0, out
                 first_product(m + 2)
             else:
                 regroup_w1(m + 2 - TILES)
-            if m < TILES:
-                nc.vector.reciprocal(out=rstd[:, m : m + 1], in_=std[:, m : m + 1])
             if m >= 1:
                 copy_out_h(m - 1)
             if m < TILES:
                 finish_h(m)
                 transpose_h(m)
+            if m == TILES - 1:
+                warm_up(ACT.Silu, rstd[:, m : m + 1])
             if m + 1 >= TILES:
                 quantise_w1(m + 1 - TILES)
             if m >= 1:

@@ -66,7 +66,7 @@ def tile_transformerblock_pa_kernel(tc, o, x_pos, Wo, bo, g1, W1, b1, out_0, out
         x_sb = keep.tile([P, TILES, E], BF16)
         b1_rows = keep.tile([P, P], BF16)
         nc.vector.memset(b1_rows[:], 0.0)
-        vec_rows = keep.tile([P, 2, E], BF16)
+        vec_rows = stage.tile([P, 2, E], BF16, tag="grp", bufs=3, align_bytes=64)
         nc.vector.memset(vec_rows[:], 0.0)
 
         nc.sync.dma_start(out=vec_rows[0:1, 0, :], in_=bo.rearrange("(a e) -> a e", a=1))
@@ -111,18 +111,19 @@ def tile_transformerblock_pa_kernel(tc, o, x_pos, Wo, bo, g1, W1, b1, out_0, out
             cols = slice(CHUNK * c, CHUNK * (c + 1))
             quantise(w1_grp[i], w1_codes[:, g, cols], w1_scales[:, g, cols])
 
-        ones = keep.tile([P, P], BF16)
-        nc.vector.memset(ones[:], 1.0)
-        ident_bf16 = keep.tile([P, P], BF16)
-        masks.make_identity(nc, ident_bf16[:])
-        g1_bc = keep.tile([P, E], BF16)
+        vec_bc = keep.tile([P, 2, E], BF16)
+        bo_bc = vec_bc[:, 0, :]
+        g1_bc = vec_bc[:, 1, :]
 
-        def spread_g1():
-            for n in range(E // BANK):
-                cols = slice(BANK * n, BANK * (n + 1))
-                spread = psum_tp.tile([P, BANK], F32, tag="tp")
-                nc.tensor.matmul(out=spread[:], lhsT=ones[:], rhs=vec_rows[:, 1, cols], start=True, stop=True)
-                nc.scalar.copy(out=g1_bc[:, cols], in_=spread[:])
+        def spread_bo_and_g1():
+            ones = keep.tile([P, P], BF16)
+            nc.vector.memset(ones[:], 1.0)
+            for v in range(2):
+                for n in range(E // BANK):
+                    cols = slice(BANK * n, BANK * (n + 1))
+                    spread = psum_tp.tile([P, BANK], F32, tag="tp")
+                    nc.tensor.matmul(out=spread[:], lhsT=ones[:], rhs=vec_rows[:, v, cols], start=True, stop=True)
+                    nc.scalar.copy(out=vec_bc[:, v, cols], in_=spread[:])
 
         def spread_b1():
             b1_rows_f32 = keep.tile([P, P], F32)
@@ -168,12 +169,7 @@ def tile_transformerblock_pa_kernel(tc, o, x_pos, Wo, bo, g1, W1, b1, out_0, out
         h_grp = {}
 
         def add_bias_to_residual(m):
-            for n in range(E // BANK):
-                cols = slice(BANK * n, BANK * (n + 1))
-                x_bo = psum_tp.tile([P, BANK], F32, tag="tp")
-                nc.tensor.matmul(out=x_bo[:], lhsT=ident_bf16[:], rhs=x_sb[:, m, cols], start=True, stop=False)
-                nc.tensor.matmul(out=x_bo[:], lhsT=ones[:], rhs=vec_rows[:, 0, cols], start=False, stop=True)
-                nc.scalar.copy(out=resid[:, m, cols], in_=x_bo[:])
+            nc.vector.tensor_tensor(out=resid[:, m, :], in0=x_sb[:, m, :], in1=bo_bc, op=ALU.add)
 
         def first_product(m):
             for n in range(E // BANK):
@@ -234,7 +230,7 @@ def tile_transformerblock_pa_kernel(tc, o, x_pos, Wo, bo, g1, W1, b1, out_0, out
                 out=h_sb[:, m, :],
                 in0=resid[:, m, :],
                 scalar=neg_mean[:, m : m + 1],
-                in1=g1_bc[:],
+                in1=g1_bc,
                 op0=ALU.add,
                 op1=ALU.mult,
             )
@@ -317,7 +313,7 @@ def tile_transformerblock_pa_kernel(tc, o, x_pos, Wo, bo, g1, W1, b1, out_0, out
             nc.scalar.activation(out=unused[:], in_=column, func=func)
 
         warm_up(ACT.Abs_reciprocal_sqrt, one[:])
-        spread_g1()
+        spread_bo_and_g1()
         spread_b1()
         wo_grp = [regroup(wo_raw[0])]
         load_w1_chunk(RAW_BUFS - PASSES)

@@ -340,8 +340,6 @@ def tile_transformerblock_pa_kernel(tc, o, x_pos, Wo, bo, g1, W1, b1, out_0, out
                 quantise_o(m + 2)
                 add_bias_to_residual(m + 2)
                 first_product(m + 2)
-            else:
-                regroup_w1(m + 2 - TILES)
             if m >= 1:
                 copy_out_h(m - 1)
             if m < TILES:
@@ -349,12 +347,13 @@ def tile_transformerblock_pa_kernel(tc, o, x_pos, Wo, bo, g1, W1, b1, out_0, out
                 transpose_h(m)
             if m == TILES - 1:
                 warm_up(ACT.Silu, rstd[:, m : m + 1])
-            if m + 1 >= TILES:
-                quantise_w1(m + 1 - TILES)
             if m >= 1:
                 quantise_h(m - 1)
-        regroup_w1(LEAD)
-        quantise_w1(LEAD - 1)
+
+        for i in range(LEAD + 1):
+            regroup_w1(i)
+            if i >= 1:
+                quantise_w1(i - 1)
 
         second_product(0)
         for j in range(ROUNDS):

@@ -22,7 +22,8 @@ PASSES = E // K_PASS
 BANK = 512
 CHUNK = 1024
 RUN = 4
-SCALAR_COLS = 256
+EARLY_COLS = 384
+LATE_COLS = 256
 ROUNDS = FF // BANK
 BLOCKS = BANK // P
 W1_CHUNKS = PASSES * FF // CHUNK
@@ -72,10 +73,16 @@ def tile_transformerblock_pa_kernel(tc, o, x_pos, Wo, bo, g1, W1, b1, out_0, out
         nc.sync.dma_start(out=vec_rows[0:1, 0, :], in_=bo.rearrange("(a e) -> a e", a=1))
         nc.sync.dma_start(out=vec_rows[0:1, 1, :], in_=g1.rearrange("(a e) -> a e", a=1))
         nc.sync.dma_start(out=b1_rows[0 : FF // P, :], in_=b1.rearrange("(c p) -> c p", p=P))
-        wo_raw = [load_wo_pass(0), load_wo_pass(1)]
-        for m in range(TILES):
-            nc.sync.dma_start(out=o_sb[:, m, :], in_=o[m, :, :])
-            nc.sync.dma_start(out=x_sb[:, m, :], in_=x_pos[m, :, :])
+        nc.sync.dma_start(out=x_sb[:, 0, :], in_=x_pos[0, :, :])
+        wo_raw = [load_wo_pass(0)]
+        nc.sync.dma_start(out=x_sb[:, 1, :], in_=x_pos[1, :, :])
+        nc.sync.dma_start(out=o_sb[:, 0, :], in_=o[0, :, :])
+        nc.sync.dma_start(out=o_sb[:, 1, :], in_=o[1, :, :])
+        wo_raw.append(load_wo_pass(1))
+        nc.sync.dma_start(out=o_sb[:, 2, :], in_=o[2, :, :])
+        nc.sync.dma_start(out=o_sb[:, 3, :], in_=o[3, :, :])
+        nc.sync.dma_start(out=x_sb[:, 2, :], in_=x_pos[2, :, :])
+        nc.sync.dma_start(out=x_sb[:, 3, :], in_=x_pos[3, :, :])
         for i in range(RAW_BUFS - PASSES):
             load_w1_chunk(i)
 
@@ -84,9 +91,9 @@ def tile_transformerblock_pa_kernel(tc, o, x_pos, Wo, bo, g1, W1, b1, out_0, out
         w1_codes = keep.tile([P, PASSES, FF], U32, align_bytes=64)
         w1_scales = keep.tile([P, PASSES, FF], U8, align_bytes=64)
 
-        def regroup(raw):
+        def regroup(raw, scalar_cols):
             grp = stage.tile([P, CHUNK, PACK], BF16, tag="grp", bufs=3, align_bytes=64)
-            split = CHUNK - SCALAR_COLS
+            split = CHUNK - scalar_cols
             nc.vector.tensor_copy(
                 out=grp[:, :split, :].rearrange("p (c i) t -> p c t i", i=RUN),
                 in_=raw[:, :, :split].rearrange("p t (c i) -> p c t i", i=RUN),
@@ -103,7 +110,7 @@ def tile_transformerblock_pa_kernel(tc, o, x_pos, Wo, bo, g1, W1, b1, out_0, out
         w1_grp = {}
 
         def regroup_w1(i):
-            w1_grp[i] = regroup(w1_raw[i])
+            w1_grp[i] = regroup(w1_raw[i], EARLY_COLS if i <= LEAD else LATE_COLS)
             load_w1_chunk(i + RAW_BUFS)
 
         def quantise_w1(i):
@@ -119,11 +126,11 @@ def tile_transformerblock_pa_kernel(tc, o, x_pos, Wo, bo, g1, W1, b1, out_0, out
             ones = keep.tile([P, P], BF16)
             nc.vector.memset(ones[:], 1.0)
             for v in range(2):
+                spread = psum_tp.tile([P, E], BF16, tag="tp")
                 for n in range(E // BANK):
                     cols = slice(BANK * n, BANK * (n + 1))
-                    spread = psum_tp.tile([P, BANK], F32, tag="tp")
-                    nc.tensor.matmul(out=spread[:], lhsT=ones[:], rhs=vec_rows[:, v, cols], start=True, stop=True)
-                    nc.scalar.copy(out=vec_bc[:, v, cols], in_=spread[:])
+                    nc.tensor.matmul(out=spread[:, cols], lhsT=ones[:], rhs=vec_rows[:, v, cols], start=True, stop=True)
+                nc.scalar.copy(out=vec_bc[:, v, :], in_=spread[:])
 
         def spread_b1():
             b1_rows_f32 = keep.tile([P, P], F32)
@@ -315,10 +322,10 @@ def tile_transformerblock_pa_kernel(tc, o, x_pos, Wo, bo, g1, W1, b1, out_0, out
         warm_up(ACT.Abs_reciprocal_sqrt, one[:])
         spread_bo_and_g1()
         spread_b1()
-        wo_grp = [regroup(wo_raw[0])]
+        wo_grp = [regroup(wo_raw[0], EARLY_COLS)]
         load_w1_chunk(RAW_BUFS - PASSES)
         quantise(wo_grp[0], wo_codes[:, 0, :], wo_scales[:, 0, :])
-        wo_grp.append(regroup(wo_raw[1]))
+        wo_grp.append(regroup(wo_raw[1], EARLY_COLS))
         load_w1_chunk(RAW_BUFS - PASSES + 1)
         for m in range(TILES):
             transpose_o(m)

@@ -21,9 +21,9 @@ FF = 4096
 PASSES = E // K_PASS
 BANK = 512
 CHUNK = 1024
-RUN = 4
-EARLY_COLS = 384
-LATE_COLS = 256
+RUN = 8
+WO_SCALAR_COLS = 512
+W1_SCALAR_COLS = 256
 ROUNDS = FF // BANK
 BLOCKS = BANK // P
 W1_CHUNKS = PASSES * FF // CHUNK
@@ -73,16 +73,10 @@ def tile_transformerblock_pa_kernel(tc, o, x_pos, Wo, bo, g1, W1, b1, out_0, out
         nc.sync.dma_start(out=vec_rows[0:1, 0, :], in_=bo.rearrange("(a e) -> a e", a=1))
         nc.sync.dma_start(out=vec_rows[0:1, 1, :], in_=g1.rearrange("(a e) -> a e", a=1))
         nc.sync.dma_start(out=b1_rows[0 : FF // P, :], in_=b1.rearrange("(c p) -> c p", p=P))
-        nc.sync.dma_start(out=x_sb[:, 0, :], in_=x_pos[0, :, :])
-        wo_raw = [load_wo_pass(0)]
-        nc.sync.dma_start(out=x_sb[:, 1, :], in_=x_pos[1, :, :])
-        nc.sync.dma_start(out=o_sb[:, 0, :], in_=o[0, :, :])
-        nc.sync.dma_start(out=o_sb[:, 1, :], in_=o[1, :, :])
-        wo_raw.append(load_wo_pass(1))
-        nc.sync.dma_start(out=o_sb[:, 2, :], in_=o[2, :, :])
-        nc.sync.dma_start(out=o_sb[:, 3, :], in_=o[3, :, :])
-        nc.sync.dma_start(out=x_sb[:, 2, :], in_=x_pos[2, :, :])
-        nc.sync.dma_start(out=x_sb[:, 3, :], in_=x_pos[3, :, :])
+        wo_raw = [load_wo_pass(0), load_wo_pass(1)]
+        for m in range(TILES):
+            nc.sync.dma_start(out=o_sb[:, m, :], in_=o[m, :, :])
+            nc.sync.dma_start(out=x_sb[:, m, :], in_=x_pos[m, :, :])
         for i in range(RAW_BUFS - PASSES):
             load_w1_chunk(i)
 
@@ -110,7 +104,7 @@ def tile_transformerblock_pa_kernel(tc, o, x_pos, Wo, bo, g1, W1, b1, out_0, out
         w1_grp = {}
 
         def regroup_w1(i):
-            w1_grp[i] = regroup(w1_raw[i], EARLY_COLS if i <= LEAD else LATE_COLS)
+            w1_grp[i] = regroup(w1_raw[i], W1_SCALAR_COLS)
             load_w1_chunk(i + RAW_BUFS)
 
         def quantise_w1(i):
@@ -322,10 +316,10 @@ def tile_transformerblock_pa_kernel(tc, o, x_pos, Wo, bo, g1, W1, b1, out_0, out
         warm_up(ACT.Abs_reciprocal_sqrt, one[:])
         spread_bo_and_g1()
         spread_b1()
-        wo_grp = [regroup(wo_raw[0], EARLY_COLS)]
+        wo_grp = [regroup(wo_raw[0], WO_SCALAR_COLS)]
         load_w1_chunk(RAW_BUFS - PASSES)
         quantise(wo_grp[0], wo_codes[:, 0, :], wo_scales[:, 0, :])
-        wo_grp.append(regroup(wo_raw[1], EARLY_COLS))
+        wo_grp.append(regroup(wo_raw[1], WO_SCALAR_COLS))
         load_w1_chunk(RAW_BUFS - PASSES + 1)
         for m in range(TILES):
             transpose_o(m)

@@ -45,6 +45,8 @@ def tile_transformerblock_pa_kernel(tc, o, x_pos, Wo, bo, g1, W1, b1, out_0, out
 
         ident = keep.tile([P, P], F32)
         masks.make_identity(nc, ident[:])
+        ident_bf = keep.tile([P, P], BF16)
+        masks.make_identity(nc, ident_bf[:])
 
         def load_wo_pass(g):
             raw = raw_pool.tile([P, PACK, CHUNK], BF16, tag="raw")
@@ -85,17 +87,31 @@ def tile_transformerblock_pa_kernel(tc, o, x_pos, Wo, bo, g1, W1, b1, out_0, out
         w1_codes = keep.tile([P, PASSES, FF], U32, align_bytes=64)
         w1_scales = keep.tile([P, PASSES, FF], U8, align_bytes=64)
 
-        def regroup(raw, scalar_cols):
+        def regroup(raw, scalar_cols, on_tensor):
             grp = stage.tile([P, CHUNK, PACK], BF16, tag="grp", bufs=3, align_bytes=64)
             split = CHUNK - scalar_cols
             nc.vector.tensor_copy(
                 out=grp[:, :split, :].rearrange("p (c i) t -> p c t i", i=RUN),
                 in_=raw[:, :, :split].rearrange("p t (c i) -> p c t i", i=RUN),
             )
-            nc.scalar.copy(
-                out=grp[:, split:, :].rearrange("p (c i) t -> p c t i", i=RUN),
-                in_=raw[:, :, split:].rearrange("p t (c i) -> p c t i", i=RUN),
-            )
+            if on_tensor:
+                moved = psum_tp.tile([P, scalar_cols, PACK], BF16, tag="tp", name="moved")
+                for c0 in range(0, scalar_cols, P):
+                    nc.tensor.matmul(
+                        out=moved[:, c0 : c0 + P, :].rearrange("p (c i) t -> p c t i", i=RUN),
+                        lhsT=ident_bf[:],
+                        rhs=raw[:, :, split + c0 : split + c0 + P].rearrange("p t (c i) -> p c t i", i=RUN),
+                        start=True,
+                        stop=True,
+                    )
+                nc.scalar.copy(
+                    out=grp[:, split:, :].rearrange("p c t -> p (c t)"), in_=moved[:].rearrange("p c t -> p (c t)")
+                )
+            else:
+                nc.scalar.copy(
+                    out=grp[:, split:, :].rearrange("p (c i) t -> p c t i", i=RUN),
+                    in_=raw[:, :, split:].rearrange("p t (c i) -> p c t i", i=RUN),
+                )
             return grp
 
         def quantise(grp, codes, scales):
@@ -104,7 +120,7 @@ def tile_transformerblock_pa_kernel(tc, o, x_pos, Wo, bo, g1, W1, b1, out_0, out
         w1_grp = {}
 
         def regroup_w1(i):
-            w1_grp[i] = regroup(w1_raw[i], W1_SCALAR_COLS)
+            w1_grp[i] = regroup(w1_raw[i], W1_SCALAR_COLS, i > LEAD)
             load_w1_chunk(i + RAW_BUFS)
 
         def quantise_w1(i):
@@ -316,10 +332,10 @@ def tile_transformerblock_pa_kernel(tc, o, x_pos, Wo, bo, g1, W1, b1, out_0, out
         warm_up(ACT.Abs_reciprocal_sqrt, one[:])
         spread_bo_and_g1()
         spread_b1()
-        wo_grp = [regroup(wo_raw[0], WO_SCALAR_COLS)]
+        wo_grp = [regroup(wo_raw[0], WO_SCALAR_COLS, False)]
         load_w1_chunk(RAW_BUFS - PASSES)
         quantise(wo_grp[0], wo_codes[:, 0, :], wo_scales[:, 0, :])
-        wo_grp.append(regroup(wo_raw[1], WO_SCALAR_COLS))
+        wo_grp.append(regroup(wo_raw[1], WO_SCALAR_COLS, False))
         load_w1_chunk(RAW_BUFS - PASSES + 1)
         for m in range(TILES):
             transpose_o(m)
@@ -364,9 +380,9 @@ def tile_transformerblock_pa_kernel(tc, o, x_pos, Wo, bo, g1, W1, b1, out_0, out
                 second_product(j + 1)
             if j >= 1:
                 store_act(j - 1, not weights_left)
-            turn_back(j)
             if weights_left:
                 quantise_w1(j + LEAD)
             if j + LEAD + 1 < W1_CHUNKS:
                 regroup_w1(j + LEAD + 1)
+            turn_back(j)
         store_act(ROUNDS - 1, True)

@@ -300,7 +300,7 @@ def tile_transformerblock_pa_kernel(tc, o, x_pos, Wo, bo, g1, W1, b1, out_0, out
                 bias = b1_col[:, BLOCKS * j + f : BLOCKS * j + f + 1]
                 sil = stage.tile([P, TOKENS], F32, tag="sil")
                 nc.scalar.activation(out=sil[:], in_=y_t[(j, f)][:], func=ACT.Silu, bias=bias, scale=1.0)
-                gated[(j, f)] = stage.tile([P, TOKENS], F32, tag="gated", bufs=6, name="gated")
+                gated[(j, f)] = stage.tile([P, TOKENS], F32, tag="gated", bufs=8, name="gated")
                 nc.vector.scalar_tensor_tensor(
                     out=gated[(j, f)][:], in0=y_t[(j, f)][:], scalar=bias, in1=sil[:], op0=ALU.add, op1=ALU.mult
                 )

from contextlib import ExitStack

import concourse.masks as masks
import concourse.mybir as mybir

F32 = mybir.dt.float32
BF16 = mybir.dt.bfloat16
U32 = mybir.dt.uint32
U8 = mybir.dt.uint8
FP8X4 = mybir.dt.float8_e4m3fn_x4
ALU = mybir.AluOpType
ACT = mybir.ActivationFunctionType

P = 128
PACK = 4
K_PASS = P * PACK
TILES = 4
TOKENS = TILES * P
E = 1024
FF = 4096
PASSES = E // K_PASS
BANK = 512
CHUNK = 1024
RUN = 8
WO_SCALAR_COLS = 512
W1_SCALAR_COLS = 256
ROUNDS = FF // BANK
BLOCKS = BANK // P
W1_CHUNKS = PASSES * FF // CHUNK
RAW_BUFS = 6
LEAD = 3
EPS = 1e-5

FLOPS = 2 * TOKENS * E * E + 2 * TOKENS * E * FF


def tile_transformerblock_pa_kernel(tc, o, x_pos, Wo, bo, g1, W1, b1, out_0, out_1):
    nc = tc.nc
    with ExitStack() as ctx:
        keep = ctx.enter_context(tc.tile_pool(name="keep", bufs=1))
        raw_pool = ctx.enter_context(tc.tile_pool(name="raw", bufs=RAW_BUFS))
        stage = ctx.enter_context(tc.tile_pool(name="stage", bufs=4))
        psum_acc = ctx.enter_context(tc.psum_pool(name="acc", bufs=4))
        psum_tp = ctx.enter_context(tc.psum_pool(name="tp", bufs=4))

        ident = keep.tile([P, P], F32)
        masks.make_identity(nc, ident[:])
        ident_bf = keep.tile([P, P], BF16)
        masks.make_identity(nc, ident_bf[:])

        def load_wo_pass(g):
            raw = raw_pool.tile([P, PACK, CHUNK], BF16, tag="raw")
            for u in range(2):
                rows = Wo[K_PASS * g + 2 * P * u : K_PASS * g + 2 * P * (u + 1), :]
                nc.sync.dma_start(out=raw[:, 2 * u : 2 * u + 2, :], in_=rows.rearrange("(q e) c -> q e c", e=2))
            return raw

        w1_raw = {}

        def load_w1_chunk(i):
            if i < W1_CHUNKS:
                c, g = divmod(i, PASSES)
                raw = raw_pool.tile([P, PACK, CHUNK], BF16, tag="raw")
                rows = W1[K_PASS * g : K_PASS * (g + 1), CHUNK * c : CHUNK * (c + 1)]
                nc.sync.dma_start(out=raw[:], in_=rows.rearrange("(t p) n -> p t n", p=P))
                w1_raw[i] = raw

        o_sb = keep.tile([P, TILES, E], BF16)
        x_sb = keep.tile([P, TILES, E], BF16)
        b1_rows = keep.tile([P, P], BF16)
        nc.vector.memset(b1_rows[:], 0.0)
        vec_rows = stage.tile([P, 2, E], BF16, tag="grp", bufs=3, align_bytes=64)
        nc.vector.memset(vec_rows[:], 0.0)

        nc.sync.dma_start(out=vec_rows[0:1, 0, :], in_=bo.rearrange("(a e) -> a e", a=1))
        nc.sync.dma_start(out=vec_rows[0:1, 1, :], in_=g1.rearrange("(a e) -> a e", a=1))
        nc.sync.dma_start(out=b1_rows[0 : FF // P, :], in_=b1.rearrange("(c p) -> c p", p=P))
        wo_raw = [load_wo_pass(0), load_wo_pass(1)]
        for m in range(TILES):
            nc.sync.dma_start(out=o_sb[:, m, :], in_=o[m, :, :])
            nc.sync.dma_start(out=x_sb[:, m, :], in_=x_pos[m, :, :])
        for i in range(RAW_BUFS - PASSES):
            load_w1_chunk(i)

        wo_codes = keep.tile([P, PASSES, E], U32, align_bytes=64)
        wo_scales = keep.tile([P, PASSES, E], U8, align_bytes=64)
        w1_codes = keep.tile([P, PASSES, FF], U32, align_bytes=64)
        w1_scales = keep.tile([P, PASSES, FF], U8, align_bytes=64)

        def regroup(raw, scalar_cols, on_tensor):
            grp = stage.tile([P, CHUNK, PACK], BF16, tag="grp", bufs=3, align_bytes=64)
            split = CHUNK - scalar_cols
            nc.vector.tensor_copy(
                out=grp[:, :split, :].rearrange("p (c i) t -> p c t i", i=RUN),
                in_=raw[:, :, :split].rearrange("p t (c i) -> p c t i", i=RUN),
            )
            if on_tensor:
                moved = psum_tp.tile([P, scalar_cols, PACK], BF16, tag="tp", name="moved")
                for c0 in range(0, scalar_cols, P):
                    nc.tensor.matmul(
                        out=moved[:, c0 : c0 + P, :].rearrange("p (c i) t -> p c t i", i=RUN),
                        lhsT=ident_bf[:],
                        rhs=raw[:, :, split + c0 : split + c0 + P].rearrange("p t (c i) -> p c t i", i=RUN),
                        start=True,
                        stop=True,
                    )
                nc.scalar.copy(
                    out=grp[:, split:, :].rearrange("p c t -> p (c t)"), in_=moved[:].rearrange("p c t -> p (c t)")
                )
            else:
                nc.scalar.copy(
                    out=grp[:, split:, :].rearrange("p (c i) t -> p c t i", i=RUN),
                    in_=raw[:, :, split:].rearrange("p t (c i) -> p c t i", i=RUN),
                )
            return grp

        def quantise(grp, codes, scales):
            nc.vector.quantize_mx(out=codes.bitcast(FP8X4), scales=scales, in_=grp[:].rearrange("p c t -> p (c t)"))

        w1_grp = {}

        def regroup_w1(i):
            w1_grp[i] = regroup(w1_raw[i], W1_SCALAR_COLS, i > LEAD)
            load_w1_chunk(i + RAW_BUFS)

        def quantise_w1(i):
            c, g = divmod(i, PASSES)
            cols = slice(CHUNK * c, CHUNK * (c + 1))
            quantise(w1_grp[i], w1_codes[:, g, cols], w1_scales[:, g, cols])

        vec_bc = keep.tile([P, 2, E], BF16)
        bo_bc = vec_bc[:, 0, :]
        g1_bc = vec_bc[:, 1, :]

        def spread_bo_and_g1():
            ones = keep.tile([P, P], BF16)
            nc.vector.memset(ones[:], 1.0)
            for v in range(2):
                spread = psum_tp.tile([P, E], BF16, tag="tp")
                for n in range(E // BANK):
                    cols = slice(BANK * n, BANK * (n + 1))
                    nc.tensor.matmul(out=spread[:, cols], lhsT=ones[:], rhs=vec_rows[:, v, cols], start=True, stop=True)
                nc.scalar.copy(out=vec_bc[:, v, :], in_=spread[:])

        def spread_b1():
            b1_rows_f32 = keep.tile([P, P], F32)
            nc.vector.tensor_copy(out=b1_rows_f32[:], in_=b1_rows[:])
            b1_t = psum_tp.tile([P, P], F32, tag="tp")
            nc.tensor.transpose(b1_t[:], b1_rows_f32[:], ident[:])
            nc.vector.tensor_copy(out=b1_col[:], in_=b1_t[:, 0 : FF // P])

        b1_col = keep.tile([P, FF // P], F32)

        o_codes = keep.tile([P, TILES, PASSES * P], U32, align_bytes=64)
        o_scales = keep.tile([P, TILES, PASSES * P], U8, align_bytes=64)
        o_t = {}
        o_grp = {}

        def transpose_o(m):
            o_words = o_sb[:, m, :].bitcast(F32)
            o_t[m] = psum_tp.tile([P, PASSES * 2, P], F32, tag="tp", name="o_t")
            for gu in range(PASSES * 2):
                nc.tensor.transpose(o_t[m][:, gu, :], o_words[:, P * gu : P * (gu + 1)], ident[:])

        def copy_out_o(m):
            o_grp[m] = stage.tile([P, PASSES, P, PACK], BF16, tag="o_grp", bufs=2, align_bytes=64, name="o_grp")
            nc.scalar.copy(out=o_grp[m][:].bitcast(F32), in_=o_t[m][:].rearrange("p (g u) r -> p g r u", u=2))

        def quantise_o(m):
            nc.vector.quantize_mx(
                out=o_codes[:, m, :].bitcast(FP8X4),
                scales=o_scales[:, m, :],
                in_=o_grp[m][:].rearrange("p g r t -> p (g r t)"),
            )

        resid = keep.tile([P, TILES, E], F32)
        h_sb = keep.tile([P, TILES, E], F32)
        row_sum = keep.tile([P, TILES * 2], F32)
        neg_mean = keep.tile([P, TILES], F32)
        sq_sum = keep.tile([P, TILES], F32)
        rstd = keep.tile([P, TILES], F32)
        h_codes = keep.tile([P, PASSES, TOKENS], U32, align_bytes=64)
        h_scales = keep.tile([P, PASSES, TOKENS], U8, align_bytes=64)
        acc = {}
        h_t = {}
        h_grp = {}

        def add_bias_to_residual(m):
            nc.vector.tensor_tensor(out=resid[:, m, :], in0=x_sb[:, m, :], in1=bo_bc, op=ALU.add)

        def first_product(m):
            for n in range(E // BANK):
                cols = slice(BANK * n, BANK * (n + 1))
                acc[(m, n)] = psum_acc.tile([P, BANK], F32, tag="acc", name="acc")
                for g in range(PASSES):
                    nc.tensor.matmul_mx(
                        out=acc[(m, n)][:],
                        lhsT=o_codes[:, m, P * g : P * (g + 1)].bitcast(FP8X4),
                        lhsT_scale=o_scales[:, m, P * g : P * (g + 1)],
                        rhs=wo_codes[:, g, cols].bitcast(FP8X4),
                        rhs_scale=wo_scales[:, g, cols],
                        start=(g == 0),
                        stop=(g == PASSES - 1),
                    )

        def residual_and_mean(m):
            for n in range(E // BANK):
                cols = slice(BANK * n, BANK * (n + 1))
                nc.vector.scalar_tensor_tensor(
                    out=resid[:, m, cols],
                    in0=acc[(m, n)][:],
                    scalar=0.0,
                    in1=resid[:, m, cols],
                    op0=ALU.add,
                    op1=ALU.add,
                    accum_out=row_sum[:, 2 * m + n : 2 * m + n + 1],
                )
            nc.vector.tensor_scalar(
                out=neg_mean[:, m : m + 1],
                in0=row_sum[:, 2 * m : 2 * m + 1],
                scalar1=row_sum[:, 2 * m + 1 : 2 * m + 2],
                scalar2=-1.0 / E,
                op0=ALU.add,
                op1=ALU.mult,
            )

        def reciprocal_deviation(m):
            squares = stage.tile([P, E], BF16, tag="squares", bufs=1)
            nc.scalar.activation(
                out=squares[:],
                in_=resid[:, m, :],
                func=ACT.Square,
                bias=neg_mean[:, m : m + 1],
                scale=1.0,
                accum_out=sq_sum[:, m : m + 1],
            )
            nc.scalar.activation(
                out=rstd[:, m : m + 1],
                in_=sq_sum[:, m : m + 1],
                func=ACT.Abs_reciprocal_sqrt,
                bias=EPS,
                scale=1.0 / E,
            )

        def centre_and_gain(m):
            nc.vector.scalar_tensor_tensor(
                out=h_sb[:, m, :],
                in0=resid[:, m, :],
                scalar=neg_mean[:, m : m + 1],
                in1=g1_bc,
                op0=ALU.add,
                op1=ALU.mult,
            )

        def finish_h(m):
            nc.scalar.activation(out=h_sb[:, m, :], in_=h_sb[:, m, :], func=ACT.Copy, scale=rstd[:, m : m + 1])
            nc.sync.dma_start(out=out_0[m, :, :], in_=h_sb[:, m, :])

        def transpose_h(m):
            for g in range(PASSES):
                h_t[(m, g)] = psum_tp.tile([P, PACK, P], F32, tag="tp", name="h_t")
                for t in range(PACK):
                    k0 = K_PASS * g + P * t
                    nc.tensor.transpose(h_t[(m, g)][:, t, :], h_sb[:, m, k0 : k0 + P], ident[:])

        def copy_out_h(m):
            for g in range(PASSES):
                h_grp[(m, g)] = stage.tile([P, P, PACK], BF16, tag="h_grp", align_bytes=64, name="h_grp")
                nc.scalar.copy(out=h_grp[(m, g)][:], in_=h_t[(m, g)][:].rearrange("p t r -> p r t"))

        def quantise_h(m):
            for g in range(PASSES):
                nc.vector.quantize_mx(
                    out=h_codes[:, g, P * m : P * (m + 1)].bitcast(FP8X4),
                    scales=h_scales[:, g, P * m : P * (m + 1)],
                    in_=h_grp[(m, g)][:].rearrange("p r t -> p (r t)"),
                )

        y_t = {}
        gated = {}
        act_t = {}

        def second_product(j):
            for f in range(BLOCKS):
                cols = slice(BANK * j + P * f, BANK * j + P * (f + 1))
                y_t[(j, f)] = psum_acc.tile([P, TOKENS], F32, tag="acc", name="y_t")
                for g in range(PASSES):
                    nc.tensor.matmul_mx(
                        out=y_t[(j, f)][:],
                        lhsT=w1_codes[:, g, cols].bitcast(FP8X4),
                        lhsT_scale=w1_scales[:, g, cols],
                        rhs=h_codes[:, g, :].bitcast(FP8X4),
                        rhs_scale=h_scales[:, g, :],
                        start=(g == 0),
                        stop=(g == PASSES - 1),
                    )

        def gate(j):
            for f in range(BLOCKS):
                bias = b1_col[:, BLOCKS * j + f : BLOCKS * j + f + 1]
                sil = stage.tile([P, TOKENS], F32, tag="sil")
                nc.scalar.activation(out=sil[:], in_=y_t[(j, f)][:], func=ACT.Silu, bias=bias, scale=1.0)
                gated[(j, f)] = stage.tile([P, TOKENS], F32, tag="gated", bufs=8, name="gated")
                nc.vector.scalar_tensor_tensor(
                    out=gated[(j, f)][:], in0=y_t[(j, f)][:], scalar=bias, in1=sil[:], op0=ALU.add, op1=ALU.mult
                )

        def turn_back(j):
            for m in range(TILES):
                act_t[(j, m)] = psum_tp.tile([P, BANK], F32, tag="tp", name="act_t")
                for f in range(BLOCKS):
                    nc.tensor.transpose(
                        act_t[(j, m)][:, P * f : P * (f + 1)], gated[(j, f)][:, P * m : P * (m + 1)], ident[:]
                    )

        def store_act(j, vector_helps):
            for m in range(TILES):
                act_sb = stage.tile([P, BANK], F32, tag="act_sb", bufs=8)
                if vector_helps and m % 2 == 1:
                    nc.vector.tensor_copy(out=act_sb[:], in_=act_t[(j, m)][:])
                else:
                    nc.scalar.copy(out=act_sb[:], in_=act_t[(j, m)][:])
                nc.sync.dma_start(out=out_1[m, :, BANK * j : BANK * (j + 1)], in_=act_sb[:])

        one = keep.tile([P, 1], F32)
        nc.vector.memset(one[:], 1.0)
        unused = keep.tile([P, 1], F32)

        def warm_up(func, column):
            nc.scalar.activation(out=unused[:], in_=column, func=func)

        warm_up(ACT.Abs_reciprocal_sqrt, one[:])
        spread_bo_and_g1()
        spread_b1()
        wo_grp = [regroup(wo_raw[0], WO_SCALAR_COLS, False)]
        load_w1_chunk(RAW_BUFS - PASSES)
        quantise(wo_grp[0], wo_codes[:, 0, :], wo_scales[:, 0, :])
        wo_grp.append(regroup(wo_raw[1], WO_SCALAR_COLS, False))
        load_w1_chunk(RAW_BUFS - PASSES + 1)
        for m in range(TILES):
            transpose_o(m)
        copy_out_o(0)
        copy_out_o(1)
        quantise(wo_grp[1], wo_codes[:, 1, :], wo_scales[:, 1, :])
        for m in range(2):
            quantise_o(m)
            add_bias_to_residual(m)
            first_product(m)
            copy_out_o(m + 2)

        for m in range(TILES + 1):
            if m < TILES:
                residual_and_mean(m)
                reciprocal_deviation(m)
                centre_and_gain(m)
            if m + 2 < TILES:
                quantise_o(m + 2)
                add_bias_to_residual(m + 2)
                first_product(m + 2)
            if m >= 1:
                copy_out_h(m - 1)
            if m < TILES:
                finish_h(m)
                transpose_h(m)
            if m == TILES - 1:
                warm_up(ACT.Silu, rstd[:, m : m + 1])
            if m >= 1:
                quantise_h(m - 1)

        for i in range(LEAD + 1):
            regroup_w1(i)
            if i >= 1:
                quantise_w1(i - 1)

        second_product(0)
        for j in range(ROUNDS):
            weights_left = j + LEAD < W1_CHUNKS
            gate(j)
            if j + 1 < ROUNDS:
                second_product(j + 1)
            if j >= 1:
                store_act(j - 1, not weights_left)
            if weights_left:
                quantise_w1(j + LEAD)
            if j + LEAD + 1 < W1_CHUNKS:
                regroup_w1(j + LEAD + 1)
            turn_back(j)
        store_act(ROUNDS - 1, True)
